import numpy as np
import ml_dtypes

BF16 = ml_dtypes.bfloat16


def bf(x):
    return np.asarray(x, np.float32).astype(BF16)


def f32(x):
    return np.asarray(x, np.float32)


def f64(x):
    return np.asarray(x).astype(np.float64)


def striped(idx):
    return np.tile(idx.reshape(-1, 16).T, (8, 1))


C, S, DEG, NH, D, H, K, N = 256, 256, 4, 2, 128, 128, 8, 1024
ALPHA = 0.2


def setup_inputs():
    idx = np.concatenate([np.random.permutation(S)[:H] for _ in range(K)])
    return {"h": f32(np.random.standard_normal((C, S))), "a_src": f32(np.random.standard_normal((C, 1)) / np.sqrt(D)), "a_dst": f32(np.random.standard_normal((C, 1)) / np.sqrt(D)), "offs": striped(idx)}


def reference(h, a_src, a_dst, offs):
    idx = offs[:16].T.reshape(-1)
    h = f64(h)
    hg = h[:, idx]
    ss = (f64(a_src) * h).reshape(NH, D, S).sum(axis=1)
    sd = (f64(a_dst) * hg).reshape(NH, D, N).sum(axis=1)
    z = sd + np.repeat(ss, DEG, axis=1)
    p = np.exp(np.maximum(z, ALPHA * z))
    num = (hg.reshape(NH, D, N) * p[:, None, :]).reshape(C, S, DEG).sum(axis=2)
    den = p.reshape(NH, S, DEG).sum(axis=2)
    v = num / np.repeat(den, D, axis=0)
    return np.maximum(v, 0.0) + np.exp(np.minimum(v, 0.0)) - 1.0

@@ -1,0 +1,104 @@
+import concourse.mybir as mybir
+
+F32 = mybir.dt.float32
+BF16 = mybir.dt.bfloat16
+U16 = mybir.dt.uint16
+ALU = mybir.AluOpType
+ACT = mybir.ActivationFunctionType
+AXIS = mybir.AxisListType
+
+P = 128
+HEADS = 2
+NODES = 256
+DEG = 4
+N = NODES * DEG
+PIECE = 256
+PIECE_NODES = PIECE // DEG
+PIECE_COLS = PIECE // 16
+SLOPE = 0.2
+
+FLOPS = 2 * 2 * HEADS * P * NODES + 2 * HEADS * P * N
+
+
+def tile_graphattentionneighbournetwork_kernel(tc, h, a_src, a_dst, offs, out):
+    nc = tc.nc
+    with (
+        tc.tile_pool(name="held", bufs=1) as held,
+        tc.tile_pool(name="work", bufs=2) as work,
+        tc.psum_pool(name="psum", bufs=2) as psum,
+    ):
+        offsets = held.tile([P, N // 16], U16, name="offsets")
+        nc.sync.dma_start(offsets[:], offs)
+
+        for n in range(HEADS):
+            rows = slice(n * P, (n + 1) * P)
+            queue = nc.sync if n == 0 else nc.scalar
+
+            h_n = work.tile([P, NODES], F32, name="h_n")
+            queue.dma_start(h_n[:], h[rows, :])
+            src_col = work.tile([P, 1], F32, name="src_col")
+            queue.dma_start(src_col[:], a_src[rows, :])
+            dst_col = work.tile([P, 1], F32, name="dst_col")
+            queue.dma_start(dst_col[:], a_dst[rows, :])
+
+            h_bf = work.tile([P, NODES], BF16, name="h_bf")
+            nc.vector.tensor_copy(h_bf[:], h_n[:])
+            src_w = work.tile([P, P], BF16, name="src_w")
+            nc.vector.tensor_copy(src_w[:], src_col[:].to_broadcast([P, P]))
+            dst_w = work.tile([P, P], BF16, name="dst_w")
+            nc.vector.tensor_copy(dst_w[:], dst_col[:].to_broadcast([P, P]))
+            ss_ps = psum.tile([P, NODES], F32, name="ss_ps")
+            nc.tensor.matmul(ss_ps[:], src_w[:], h_bf[:], start=True, stop=True)
+            sdn_ps = psum.tile([P, NODES], F32, name="sdn_ps")
+            nc.tensor.matmul(sdn_ps[:], dst_w[:], h_bf[:], start=True, stop=True)
+            ss_rep = work.tile([P, NODES, DEG], F32, name="ss_rep")
+            nc.scalar.copy(ss_rep[:], ss_ps[:].unsqueeze(2).to_broadcast([P, NODES, DEG]))
+            sdn = work.tile([P, NODES], F32, name="sdn")
+            nc.vector.tensor_copy(sdn[:], sdn_ps[:])
+
+            z = work.tile([P, NODES, DEG], F32, name="z")
+            for q in range(N // PIECE):
+                nodes = slice(q * PIECE_NODES, (q + 1) * PIECE_NODES)
+                nc.vector.tensor_tensor(
+                    z[:, nodes, :],
+                    sdn[:].indirect(offsets[:, q * PIECE_COLS : (q + 1) * PIECE_COLS]),
+                    ss_rep[:, nodes, :],
+                    ALU.add,
+                )
+
+            lrelu = work.tile([P, NODES, DEG], F32, name="lrelu")
+            nc.vector.scalar_tensor_tensor(lrelu[:], z[:], SLOPE, z[:], op0=ALU.mult, op1=ALU.max)
+            top = work.tile([P, NODES], F32, name="top")
+            nc.vector.tensor_reduce(top[:], lrelu[:], axis=AXIS.X, op=ALU.max)
+            shifted = work.tile([P, NODES, DEG], F32, name="shifted")
+            nc.vector.tensor_tensor(
+                shifted[:], lrelu[:], top[:].unsqueeze(2).to_broadcast([P, NODES, DEG]), ALU.subtract
+            )
+            p = work.tile([P, NODES, DEG], F32, name="p")
+            nc.scalar.activation(p[:], shifted[:], ACT.Exp)
+            den = work.tile([P, NODES], F32, name="den")
+            nc.vector.tensor_reduce(den[:], p[:], axis=AXIS.X, op=ALU.add)
+            inv_den = work.tile([P, NODES], F32, name="inv_den")
+            nc.vector.reciprocal(inv_den[:], den[:])
+
+            prod = work.tile([P, NODES, DEG], F32, name="prod")
+            for q in range(N // PIECE):
+                nodes = slice(q * PIECE_NODES, (q + 1) * PIECE_NODES)
+                nc.vector.tensor_tensor(
+                    prod[:, nodes, :],
+                    h_n[:].indirect(offsets[:, q * PIECE_COLS : (q + 1) * PIECE_COLS]),
+                    p[:, nodes, :],
+                    ALU.mult,
+                )
+            num = work.tile([P, NODES], F32, name="num")
+            nc.vector.tensor_reduce(num[:], prod[:], axis=AXIS.X, op=ALU.add)
+            v = work.tile([P, NODES], F32, name="v")
+            nc.vector.tensor_tensor(v[:], num[:], inv_den[:], ALU.mult)
+
+            v_neg = work.tile([P, NODES], F32, name="v_neg")
+            nc.vector.tensor_scalar_min(v_neg[:], v[:], 0.0)
+            exp_neg = work.tile([P, NODES], F32, name="exp_neg")
+            nc.scalar.activation(exp_neg[:], v_neg[:], ACT.Exp)
+            elu = work.tile([P, NODES], F32, name="elu")
+            nc.vector.scalar_tensor_tensor(elu[:], exp_neg[:], -1.0, v[:], op0=ALU.add, op1=ALU.max)
+            queue.dma_start(out[rows, :], elu[:])

@@ -1,4 +1,5 @@
 import concourse.mybir as mybir
+from concourse.masks import make_identity
 
 F32 = mybir.dt.float32
 BF16 = mybir.dt.bfloat16
@@ -9,12 +10,16 @@ AXIS = mybir.AxisListType
 
 P = 128
 HEADS = 2
+HALF = P // HEADS
 NODES = 256
+BLOCKS = NODES // P
 DEG = 4
 N = NODES * DEG
 PIECE = 256
+PIECES = N // PIECE
 PIECE_NODES = PIECE // DEG
 PIECE_COLS = PIECE // 16
+BLOCK_PIECES = PIECES // BLOCKS
 SLOPE = 0.2
 
 FLOPS = 2 * 2 * HEADS * P * NODES + 2 * HEADS * P * N
@@ -24,81 +29,117 @@ def tile_graphattentionneighbournetwork_kernel(tc, h, a_src, a_dst, offs, out):
     nc = tc.nc
     with (
         tc.tile_pool(name="held", bufs=1) as held,
+        tc.tile_pool(name="small", bufs=2) as small,
         tc.tile_pool(name="work", bufs=2) as work,
-        tc.psum_pool(name="psum", bufs=2) as psum,
+        tc.psum_pool(name="sums", bufs=1) as sums,
+        tc.psum_pool(name="turned", bufs=BLOCKS) as turned,
+        tc.psum_pool(name="spread", bufs=BLOCKS * HEADS) as spread,
     ):
         offsets = held.tile([P, N // 16], U16, name="offsets")
         nc.sync.dma_start(offsets[:], offs)
 
+        def piece(q):
+            return offsets[:, q * PIECE_COLS : (q + 1) * PIECE_COLS]
+
+        h_sb, src_col, dst_col = [], [], []
         for n in range(HEADS):
             rows = slice(n * P, (n + 1) * P)
             queue = nc.sync if n == 0 else nc.scalar
+            h_sb.append(held.tile([P, NODES], F32, name=f"h{n}"))
+            queue.dma_start(h_sb[n][:], h[rows, :])
+            src_col.append(held.tile([P, 1], F32, name=f"src_col{n}"))
+            queue.dma_start(src_col[n][:], a_src[rows, :])
+            dst_col.append(held.tile([P, 1], F32, name=f"dst_col{n}"))
+            queue.dma_start(dst_col[n][:], a_dst[rows, :])
 
-            h_n = work.tile([P, NODES], F32, name="h_n")
-            queue.dma_start(h_n[:], h[rows, :])
-            src_col = work.tile([P, 1], F32, name="src_col")
-            queue.dma_start(src_col[:], a_src[rows, :])
-            dst_col = work.tile([P, 1], F32, name="dst_col")
-            queue.dma_start(dst_col[:], a_dst[rows, :])
+        ident = held.tile([P, P], F32, name="ident")
+        make_identity(nc, ident[:])
 
-            h_bf = work.tile([P, NODES], BF16, name="h_bf")
-            nc.vector.tensor_copy(h_bf[:], h_n[:])
-            src_w = work.tile([P, P], BF16, name="src_w")
-            nc.vector.tensor_copy(src_w[:], src_col[:].to_broadcast([P, P]))
-            dst_w = work.tile([P, P], BF16, name="dst_w")
-            nc.vector.tensor_copy(dst_w[:], dst_col[:].to_broadcast([P, P]))
-            ss_ps = psum.tile([P, NODES], F32, name="ss_ps")
-            nc.tensor.matmul(ss_ps[:], src_w[:], h_bf[:], start=True, stop=True)
-            sdn_ps = psum.tile([P, NODES], F32, name="sdn_ps")
-            nc.tensor.matmul(sdn_ps[:], dst_w[:], h_bf[:], start=True, stop=True)
-            ss_rep = work.tile([P, NODES, DEG], F32, name="ss_rep")
-            nc.scalar.copy(ss_rep[:], ss_ps[:].unsqueeze(2).to_broadcast([P, NODES, DEG]))
-            sdn = work.tile([P, NODES], F32, name="sdn")
-            nc.vector.tensor_copy(sdn[:], sdn_ps[:])
+        src_w = held.tile([P, HEADS, P], BF16, name="src_w")
+        dst_w = held.tile([P, HEADS, P], BF16, name="dst_w")
+        nc.vector.memset(src_w[:], 0.0)
+        nc.vector.memset(dst_w[:], 0.0)
+        for n in range(HEADS):
+            half = slice(n * HALF, (n + 1) * HALF)
+            nc.vector.tensor_copy(src_w[:, n, half], src_col[n][:].to_broadcast([P, HALF]))
+            nc.vector.tensor_copy(dst_w[:, n, half], dst_col[n][:].to_broadcast([P, HALF]))
 
-            z = work.tile([P, NODES, DEG], F32, name="z")
-            for q in range(N // PIECE):
-                nodes = slice(q * PIECE_NODES, (q + 1) * PIECE_NODES)
-                nc.vector.tensor_tensor(
-                    z[:, nodes, :],
-                    sdn[:].indirect(offsets[:, q * PIECE_COLS : (q + 1) * PIECE_COLS]),
-                    ss_rep[:, nodes, :],
-                    ALU.add,
-                )
+        h_bf = [held.tile([P, NODES], BF16, name=f"h_bf{n}") for n in range(HEADS)]
+        nc.vector.tensor_copy(h_bf[0][:], h_sb[0][:])
+        nc.scalar.copy(h_bf[1][:], h_sb[1][:])
 
-            lrelu = work.tile([P, NODES, DEG], F32, name="lrelu")
-            nc.vector.scalar_tensor_tensor(lrelu[:], z[:], SLOPE, z[:], op0=ALU.mult, op1=ALU.max)
-            top = work.tile([P, NODES], F32, name="top")
-            nc.vector.tensor_reduce(top[:], lrelu[:], axis=AXIS.X, op=ALU.max)
-            shifted = work.tile([P, NODES, DEG], F32, name="shifted")
-            nc.vector.tensor_tensor(
-                shifted[:], lrelu[:], top[:].unsqueeze(2).to_broadcast([P, NODES, DEG]), ALU.subtract
+        ss_ps = sums.tile([P, NODES], F32, name="ss_ps")
+        for n in range(HEADS):
+            nc.tensor.matmul(ss_ps[:], src_w[:, n, :], h_bf[n][:], start=(n == 0), stop=(n == HEADS - 1))
+        sdn_ps = sums.tile([P, NODES], F32, name="sdn_ps")
+        for n in range(HEADS):
+            nc.tensor.matmul(sdn_ps[:], dst_w[:, n, :], h_bf[n][:], start=(n == 0), stop=(n == HEADS - 1))
+        sdn = held.tile([P, NODES], F32, name="sdn")
+        nc.vector.tensor_copy(sdn[:], sdn_ps[:])
+
+        ss_rep = held.tile([P, NODES, DEG], F32, name="ss_rep")
+        z = held.tile([P, NODES, DEG], F32, name="z")
+        for q in range(PIECES):
+            nodes = slice(q * PIECE_NODES, (q + 1) * PIECE_NODES)
+            nc.scalar.copy(
+                ss_rep[:, nodes, :], ss_ps[:, nodes].unsqueeze(2).to_broadcast([P, PIECE_NODES, DEG])
             )
-            p = work.tile([P, NODES, DEG], F32, name="p")
+            nc.vector.tensor_tensor(z[:, nodes, :], sdn[:].indirect(piece(q)), ss_rep[:, nodes, :], ALU.add)
+
+        for b in range(BLOCKS):
+            block = slice(b * P, (b + 1) * P)
+
+            z_t = turned.tile([P, DEG, HEADS, HALF], F32, name="z_t")
+            for d in range(DEG):
+                nc.tensor.transpose(z_t[:, d, :, :].rearrange("i n k -> i (n k)"), z[:, block, d], ident[:])
+            scores = z_t[:, :, :, 0].rearrange("i d n -> i n d")
+
+            scaled = small.tile([P, HEADS, DEG], F32, name="scaled")
+            nc.vector.tensor_scalar_mul(scaled[:], scores, SLOPE)
+            lrelu = small.tile([P, HEADS, DEG], F32, name="lrelu")
+            nc.vector.tensor_tensor(lrelu[:], scaled[:], scores, ALU.max)
+            top = small.tile([P, HEADS], F32, name="top")
+            nc.vector.tensor_reduce(top[:], lrelu[:], axis=AXIS.X, op=ALU.max)
+            shifted = small.tile([P, HEADS, DEG], F32, name="shifted")
+            nc.vector.tensor_tensor(
+                shifted[:], lrelu[:], top[:].unsqueeze(2).to_broadcast([P, HEADS, DEG]), ALU.subtract
+            )
+            p = small.tile([P, HEADS, DEG], F32, name="p")
             nc.scalar.activation(p[:], shifted[:], ACT.Exp)
-            den = work.tile([P, NODES], F32, name="den")
+            den = small.tile([P, HEADS], F32, name="den")
             nc.vector.tensor_reduce(den[:], p[:], axis=AXIS.X, op=ALU.add)
-            inv_den = work.tile([P, NODES], F32, name="inv_den")
+            inv_den = small.tile([P, HEADS], F32, name="inv_den")
             nc.vector.reciprocal(inv_den[:], den[:])
+            weight = small.tile([P, HEADS, DEG], F32, name="weight")
+            nc.vector.tensor_tensor(
+                weight[:], p[:], inv_den[:].unsqueeze(2).to_broadcast([P, HEADS, DEG]), ALU.mult
+            )
 
-            prod = work.tile([P, NODES, DEG], F32, name="prod")
-            for q in range(N // PIECE):
-                nodes = slice(q * PIECE_NODES, (q + 1) * PIECE_NODES)
-                nc.vector.tensor_tensor(
-                    prod[:, nodes, :],
-                    h_n[:].indirect(offsets[:, q * PIECE_COLS : (q + 1) * PIECE_COLS]),
-                    p[:, nodes, :],
-                    ALU.mult,
-                )
-            num = work.tile([P, NODES], F32, name="num")
-            nc.vector.tensor_reduce(num[:], prod[:], axis=AXIS.X, op=ALU.add)
-            v = work.tile([P, NODES], F32, name="v")
-            nc.vector.tensor_tensor(v[:], num[:], inv_den[:], ALU.mult)
+            for n in range(HEADS):
+                spread_ps = spread.tile([P, DEG, P], F32, name="spread_ps")
+                for d in range(DEG):
+                    nc.tensor.transpose(
+                        spread_ps[:, d, :], weight[:, n, d : d + 1].to_broadcast([P, P]), ident[:]
+                    )
+                w_rows = work.tile([P, P, DEG], F32, name="w_rows")
+                nc.scalar.copy(w_rows[:], spread_ps[:].rearrange("c d i -> c i d"))
 
-            v_neg = work.tile([P, NODES], F32, name="v_neg")
-            nc.vector.tensor_scalar_min(v_neg[:], v[:], 0.0)
-            exp_neg = work.tile([P, NODES], F32, name="exp_neg")
-            nc.scalar.activation(exp_neg[:], v_neg[:], ACT.Exp)
-            elu = work.tile([P, NODES], F32, name="elu")
-            nc.vector.scalar_tensor_tensor(elu[:], exp_neg[:], -1.0, v[:], op0=ALU.add, op1=ALU.max)
-            queue.dma_start(out[rows, :], elu[:])
+                prod = work.tile([P, P, DEG], F32, name="prod")
+                for k in range(BLOCK_PIECES):
+                    nodes = slice(k * PIECE_NODES, (k + 1) * PIECE_NODES)
+                    nc.vector.tensor_tensor(
+                        prod[:, nodes, :],
+                        h_sb[n][:].indirect(piece(b * BLOCK_PIECES + k)),
+                        w_rows[:, nodes, :],
+                        ALU.mult,
+                    )
+                v = work.tile([P, P], F32, name="v")
+                nc.vector.tensor_reduce(v[:], prod[:], axis=AXIS.X, op=ALU.add)
+
+                relu_neg = work.tile([P, P], F32, name="relu_neg")
+                nc.scalar.activation(relu_neg[:], v[:], ACT.Relu, scale=-1.0)
+                exp_neg = work.tile([P, P], F32, name="exp_neg")
+                nc.scalar.activation(exp_neg[:], relu_neg[:], ACT.Exp, scale=-1.0)
+                elu = work.tile([P, P], F32, name="elu")
+                nc.vector.scalar_tensor_tensor(elu[:], exp_neg[:], -1.0, v[:], op0=ALU.add, op1=ALU.max)
+                nc.sync.dma_start(out[n * P : (n + 1) * P, block], elu[:])

@@ -29,85 +29,81 @@ def tile_graphattentionneighbournetwork_kernel(tc, h, a_src, a_dst, offs, out):
     nc = tc.nc
     with (
         tc.tile_pool(name="held", bufs=1) as held,
-        tc.tile_pool(name="small", bufs=2) as small,
-        tc.tile_pool(name="work", bufs=2) as work,
+        tc.tile_pool(name="small", bufs=BLOCKS) as small,
+        tc.tile_pool(name="work", bufs=BLOCKS * HEADS) as work,
         tc.psum_pool(name="sums", bufs=1) as sums,
         tc.psum_pool(name="turned", bufs=BLOCKS) as turned,
         tc.psum_pool(name="spread", bufs=BLOCKS * HEADS) as spread,
     ):
+        h_sb = [held.tile([P, NODES], F32, name=f"h{n}") for n in range(HEADS)]
+        nc.sync.dma_start(h_sb[0][:], h[0:P, :])
+        nc.scalar.dma_start(h_sb[1][:], h[P : 2 * P, :])
         offsets = held.tile([P, N // 16], U16, name="offsets")
         nc.sync.dma_start(offsets[:], offs)
+        src_cols = held.tile([P, HEADS], F32, name="src_cols")
+        dst_cols = held.tile([P, HEADS], F32, name="dst_cols")
+        with nc.allow_non_contiguous_dma(reason="256 floats, one to a partition and head"):
+            nc.sync.dma_start(src_cols[:], a_src.rearrange("(n c) o -> c (n o)", n=HEADS))
+            nc.scalar.dma_start(dst_cols[:], a_dst.rearrange("(n c) o -> c (n o)", n=HEADS))
 
         def piece(q):
             return offsets[:, q * PIECE_COLS : (q + 1) * PIECE_COLS]
 
-        h_sb, src_col, dst_col = [], [], []
-        for n in range(HEADS):
-            rows = slice(n * P, (n + 1) * P)
-            queue = nc.sync if n == 0 else nc.scalar
-            h_sb.append(held.tile([P, NODES], F32, name=f"h{n}"))
-            queue.dma_start(h_sb[n][:], h[rows, :])
-            src_col.append(held.tile([P, 1], F32, name=f"src_col{n}"))
-            queue.dma_start(src_col[n][:], a_src[rows, :])
-            dst_col.append(held.tile([P, 1], F32, name=f"dst_col{n}"))
-            queue.dma_start(dst_col[n][:], a_dst[rows, :])
-
         ident = held.tile([P, P], F32, name="ident")
         make_identity(nc, ident[:])
 
-        src_w = held.tile([P, HEADS, P], BF16, name="src_w")
-        dst_w = held.tile([P, HEADS, P], BF16, name="dst_w")
-        nc.vector.memset(src_w[:], 0.0)
-        nc.vector.memset(dst_w[:], 0.0)
-        for n in range(HEADS):
-            half = slice(n * HALF, (n + 1) * HALF)
-            nc.vector.tensor_copy(src_w[:, n, half], src_col[n][:].to_broadcast([P, HALF]))
-            nc.vector.tensor_copy(dst_w[:, n, half], dst_col[n][:].to_broadcast([P, HALF]))
-
+        src_w = held.tile([P, HEADS, HALF], BF16, name="src_w")
+        nc.vector.tensor_copy(src_w[:], src_cols[:].unsqueeze(2).to_broadcast([P, HEADS, HALF]))
+        dst_w = held.tile([P, HEADS, HALF], BF16, name="dst_w")
+        nc.vector.tensor_copy(dst_w[:], dst_cols[:].unsqueeze(2).to_broadcast([P, HEADS, HALF]))
         h_bf = [held.tile([P, NODES], BF16, name=f"h_bf{n}") for n in range(HEADS)]
         nc.vector.tensor_copy(h_bf[0][:], h_sb[0][:])
         nc.scalar.copy(h_bf[1][:], h_sb[1][:])
 
         ss_ps = sums.tile([P, NODES], F32, name="ss_ps")
-        for n in range(HEADS):
-            nc.tensor.matmul(ss_ps[:], src_w[:, n, :], h_bf[n][:], start=(n == 0), stop=(n == HEADS - 1))
         sdn_ps = sums.tile([P, NODES], F32, name="sdn_ps")
         for n in range(HEADS):
-            nc.tensor.matmul(sdn_ps[:], dst_w[:, n, :], h_bf[n][:], start=(n == 0), stop=(n == HEADS - 1))
+            half = slice(n * HALF, (n + 1) * HALF)
+            nc.tensor.matmul(ss_ps[half, :], src_w[:, n, :], h_bf[n][:], start=True, stop=True)
+        for n in range(HEADS):
+            half = slice(n * HALF, (n + 1) * HALF)
+            nc.tensor.matmul(sdn_ps[half, :], dst_w[:, n, :], h_bf[n][:], start=True, stop=True)
         sdn = held.tile([P, NODES], F32, name="sdn")
         nc.vector.tensor_copy(sdn[:], sdn_ps[:])
 
-        ss_rep = held.tile([P, NODES, DEG], F32, name="ss_rep")
-        z = held.tile([P, NODES, DEG], F32, name="z")
+        z = [held.tile([P, P, DEG], F32, name=f"z{b}") for b in range(BLOCKS)]
         for q in range(PIECES):
-            nodes = slice(q * PIECE_NODES, (q + 1) * PIECE_NODES)
+            b, k = divmod(q, BLOCK_PIECES)
+            ss_rep = work.tile([P, PIECE_NODES, DEG], F32, name="ss_rep")
             nc.scalar.copy(
-                ss_rep[:, nodes, :], ss_ps[:, nodes].unsqueeze(2).to_broadcast([P, PIECE_NODES, DEG])
+                ss_rep[:],
+                ss_ps[:, q * PIECE_NODES : (q + 1) * PIECE_NODES].unsqueeze(2).to_broadcast([P, PIECE_NODES, DEG]),
             )
-            nc.vector.tensor_tensor(z[:, nodes, :], sdn[:].indirect(piece(q)), ss_rep[:, nodes, :], ALU.add)
+            nc.vector.tensor_tensor(
+                z[b][:, k * PIECE_NODES : (k + 1) * PIECE_NODES, :], sdn[:].indirect(piece(q)), ss_rep[:], ALU.add
+            )
 
+        w_rows = {}
         for b in range(BLOCKS):
-            block = slice(b * P, (b + 1) * P)
-
             z_t = turned.tile([P, DEG, HEADS, HALF], F32, name="z_t")
             for d in range(DEG):
-                nc.tensor.transpose(z_t[:, d, :, :].rearrange("i n k -> i (n k)"), z[:, block, d], ident[:])
+                nc.tensor.transpose(z_t[:, d, :, :].rearrange("i n k -> i (n k)"), z[b][:, :, d], ident[:])
             scores = z_t[:, :, :, 0].rearrange("i d n -> i n d")
 
             scaled = small.tile([P, HEADS, DEG], F32, name="scaled")
             nc.vector.tensor_scalar_mul(scaled[:], scores, SLOPE)
+            neg_max = small.tile([P, HEADS], F32, name="neg_max")
+            nc.vector.tensor_reduce(neg_max[:], scores, axis=AXIS.X, op=ALU.max, negate=True)
             lrelu = small.tile([P, HEADS, DEG], F32, name="lrelu")
             nc.vector.tensor_tensor(lrelu[:], scaled[:], scores, ALU.max)
-            top = small.tile([P, HEADS], F32, name="top")
-            nc.vector.tensor_reduce(top[:], lrelu[:], axis=AXIS.X, op=ALU.max)
-            shifted = small.tile([P, HEADS, DEG], F32, name="shifted")
-            nc.vector.tensor_tensor(
-                shifted[:], lrelu[:], top[:].unsqueeze(2).to_broadcast([P, HEADS, DEG]), ALU.subtract
-            )
+            neg_top = small.tile([P, HEADS], F32, name="neg_top")
+            nc.vector.scalar_tensor_tensor(neg_top[:], neg_max[:], SLOPE, neg_max[:], op0=ALU.mult, op1=ALU.min)
             p = small.tile([P, HEADS, DEG], F32, name="p")
-            nc.scalar.activation(p[:], shifted[:], ACT.Exp)
             den = small.tile([P, HEADS], F32, name="den")
-            nc.vector.tensor_reduce(den[:], p[:], axis=AXIS.X, op=ALU.add)
+            for n in range(HEADS):
+                nc.scalar.activation(
+                    p[:, n, :], lrelu[:, n, :], ACT.Exp, bias=neg_top[:, n : n + 1], accum_out=den[:, n : n + 1]
+                )
             inv_den = small.tile([P, HEADS], F32, name="inv_den")
             nc.vector.reciprocal(inv_den[:], den[:])
             weight = small.tile([P, HEADS, DEG], F32, name="weight")
@@ -121,16 +117,20 @@ def tile_graphattentionneighbournetwork_kernel(tc, h, a_src, a_dst, offs, out):
                     nc.tensor.transpose(
                         spread_ps[:, d, :], weight[:, n, d : d + 1].to_broadcast([P, P]), ident[:]
                     )
-                w_rows = work.tile([P, P, DEG], F32, name="w_rows")
-                nc.scalar.copy(w_rows[:], spread_ps[:].rearrange("c d i -> c i d"))
+                w_rows[b, n] = work.tile([P, P, DEG], F32, name="w_rows")
+                for k in range(BLOCK_PIECES):
+                    nodes = slice(k * PIECE_NODES, (k + 1) * PIECE_NODES)
+                    nc.scalar.copy(w_rows[b, n][:, nodes, :], spread_ps[:, :, nodes].rearrange("c d i -> c i d"))
 
+        for b in range(BLOCKS):
+            for n in range(HEADS):
                 prod = work.tile([P, P, DEG], F32, name="prod")
                 for k in range(BLOCK_PIECES):
                     nodes = slice(k * PIECE_NODES, (k + 1) * PIECE_NODES)
                     nc.vector.tensor_tensor(
                         prod[:, nodes, :],
                         h_sb[n][:].indirect(piece(b * BLOCK_PIECES + k)),
-                        w_rows[:, nodes, :],
+                        w_rows[b, n][:, nodes, :],
                         ALU.mult,
                     )
                 v = work.tile([P, P], F32, name="v")
@@ -142,4 +142,4 @@ def tile_graphattentionneighbournetwork_kernel(tc, h, a_src, a_dst, offs, out):
                 nc.scalar.activation(exp_neg[:], relu_neg[:], ACT.Exp, scale=-1.0)
                 elu = work.tile([P, P], F32, name="elu")
                 nc.vector.scalar_tensor_tensor(elu[:], exp_neg[:], -1.0, v[:], op0=ALU.add, op1=ALU.max)
-                nc.sync.dma_start(out[n * P : (n + 1) * P, block], elu[:])
+                nc.sync.dma_start(out[n * P : (n + 1) * P, b * P : (b + 1) * P], elu[:])

@@ -31,9 +31,7 @@ def tile_graphattentionneighbournetwork_kernel(tc, h, a_src, a_dst, offs, out):
         tc.tile_pool(name="held", bufs=1) as held,
         tc.tile_pool(name="small", bufs=BLOCKS) as small,
         tc.tile_pool(name="work", bufs=BLOCKS * HEADS) as work,
-        tc.psum_pool(name="sums", bufs=1) as sums,
-        tc.psum_pool(name="turned", bufs=BLOCKS) as turned,
-        tc.psum_pool(name="spread", bufs=BLOCKS * HEADS) as spread,
+        tc.psum_pool(name="psum", bufs=2) as psum,
     ):
         h_sb = [held.tile([P, NODES], F32, name=f"h{n}") for n in range(HEADS)]
         nc.sync.dma_start(h_sb[0][:], h[0:P, :])
@@ -60,8 +58,8 @@ def tile_graphattentionneighbournetwork_kernel(tc, h, a_src, a_dst, offs, out):
         nc.vector.tensor_copy(h_bf[0][:], h_sb[0][:])
         nc.scalar.copy(h_bf[1][:], h_sb[1][:])
 
-        ss_ps = sums.tile([P, NODES], F32, name="ss_ps")
-        sdn_ps = sums.tile([P, NODES], F32, name="sdn_ps")
+        sums_ps = psum.tile([P, 2, NODES], F32, name="sums_ps", bufs=1)
+        ss_ps, sdn_ps = sums_ps[:, 0, :], sums_ps[:, 1, :]
         for n in range(HEADS):
             half = slice(n * HALF, (n + 1) * HALF)
             nc.tensor.matmul(ss_ps[half, :], src_w[:, n, :], h_bf[n][:], start=True, stop=True)
@@ -69,7 +67,7 @@ def tile_graphattentionneighbournetwork_kernel(tc, h, a_src, a_dst, offs, out):
             half = slice(n * HALF, (n + 1) * HALF)
             nc.tensor.matmul(sdn_ps[half, :], dst_w[:, n, :], h_bf[n][:], start=True, stop=True)
         sdn = held.tile([P, NODES], F32, name="sdn")
-        nc.vector.tensor_copy(sdn[:], sdn_ps[:])
+        nc.vector.tensor_copy(sdn[:], sdn_ps)
 
         z = [held.tile([P, P, DEG], F32, name=f"z{b}") for b in range(BLOCKS)]
         for q in range(PIECES):
@@ -83,9 +81,9 @@ def tile_graphattentionneighbournetwork_kernel(tc, h, a_src, a_dst, offs, out):
                 z[b][:, k * PIECE_NODES : (k + 1) * PIECE_NODES, :], sdn[:].indirect(piece(q)), ss_rep[:], ALU.add
             )
 
-        w_rows = {}
+        p_rows, inv_den, neg_inv_den = {}, [], []
         for b in range(BLOCKS):
-            z_t = turned.tile([P, DEG, HEADS, HALF], F32, name="z_t")
+            z_t = psum.tile([P, DEG, HEADS, HALF], F32, name="z_t")
             for d in range(DEG):
                 nc.tensor.transpose(z_t[:, d, :, :].rearrange("i n k -> i (n k)"), z[b][:, :, d], ident[:])
             scores = z_t[:, :, :, 0].rearrange("i d n -> i n d")
@@ -104,23 +102,19 @@ def tile_graphattentionneighbournetwork_kernel(tc, h, a_src, a_dst, offs, out):
                 nc.scalar.activation(
                     p[:, n, :], lrelu[:, n, :], ACT.Exp, bias=neg_top[:, n : n + 1], accum_out=den[:, n : n + 1]
                 )
-            inv_den = small.tile([P, HEADS], F32, name="inv_den")
-            nc.vector.reciprocal(inv_den[:], den[:])
-            weight = small.tile([P, HEADS, DEG], F32, name="weight")
-            nc.vector.tensor_tensor(
-                weight[:], p[:], inv_den[:].unsqueeze(2).to_broadcast([P, HEADS, DEG]), ALU.mult
-            )
+            inv_den.append(small.tile([P, HEADS], F32, name="inv_den"))
+            nc.vector.reciprocal(inv_den[b][:], den[:])
+            neg_inv_den.append(small.tile([P, HEADS], F32, name="neg_inv_den"))
+            nc.vector.tensor_scalar_mul(neg_inv_den[b][:], inv_den[b][:], -1.0)
 
             for n in range(HEADS):
-                spread_ps = spread.tile([P, DEG, P], F32, name="spread_ps")
+                spread_ps = psum.tile([P, DEG, P], F32, name="spread_ps")
                 for d in range(DEG):
-                    nc.tensor.transpose(
-                        spread_ps[:, d, :], weight[:, n, d : d + 1].to_broadcast([P, P]), ident[:]
-                    )
-                w_rows[b, n] = work.tile([P, P, DEG], F32, name="w_rows")
+                    nc.tensor.transpose(spread_ps[:, d, :], p[:, n, d : d + 1].to_broadcast([P, P]), ident[:])
+                p_rows[b, n] = work.tile([P, P, DEG], F32, name="p_rows")
                 for k in range(BLOCK_PIECES):
                     nodes = slice(k * PIECE_NODES, (k + 1) * PIECE_NODES)
-                    nc.scalar.copy(w_rows[b, n][:, nodes, :], spread_ps[:, :, nodes].rearrange("c d i -> c i d"))
+                    nc.scalar.copy(p_rows[b, n][:, nodes, :], spread_ps[:, :, nodes].rearrange("c d i -> c i d"))
 
         for b in range(BLOCKS):
             for n in range(HEADS):
@@ -130,16 +124,25 @@ def tile_graphattentionneighbournetwork_kernel(tc, h, a_src, a_dst, offs, out):
                     nc.vector.tensor_tensor(
                         prod[:, nodes, :],
                         h_sb[n][:].indirect(piece(b * BLOCK_PIECES + k)),
-                        w_rows[b, n][:, nodes, :],
+                        p_rows[b, n][:, nodes, :],
                         ALU.mult,
                     )
-                v = work.tile([P, P], F32, name="v")
-                nc.vector.tensor_reduce(v[:], prod[:], axis=AXIS.X, op=ALU.add)
+                num_t = psum.tile([P, P], F32, name="num_t")
+                for d in range(DEG):
+                    nc.tensor.matmul(
+                        num_t[:], prod[:, :, d], ident[:], start=(d == 0), stop=(d == DEG - 1), is_transpose=True
+                    )
 
+                relu_pos = work.tile([P, P], F32, name="relu_pos")
+                nc.scalar.activation(relu_pos[:], num_t[:], ACT.Relu, scale=inv_den[b][:, n : n + 1])
                 relu_neg = work.tile([P, P], F32, name="relu_neg")
-                nc.scalar.activation(relu_neg[:], v[:], ACT.Relu, scale=-1.0)
+                nc.scalar.activation(relu_neg[:], num_t[:], ACT.Relu, scale=neg_inv_den[b][:, n : n + 1])
                 exp_neg = work.tile([P, P], F32, name="exp_neg")
                 nc.scalar.activation(exp_neg[:], relu_neg[:], ACT.Exp, scale=-1.0)
+
+                elu_ps = psum.tile([P, P], F32, name="elu_ps", bufs=1)
+                nc.tensor.matmul(elu_ps[:], relu_pos[:], ident[:], start=True, stop=False, is_transpose=True)
+                nc.tensor.matmul(elu_ps[:], exp_neg[:], ident[:], start=False, stop=True, is_transpose=True)
                 elu = work.tile([P, P], F32, name="elu")
-                nc.vector.scalar_tensor_tensor(elu[:], exp_neg[:], -1.0, v[:], op0=ALU.add, op1=ALU.max)
+                nc.scalar.add(elu[:], elu_ps[:], -1.0)
                 nc.sync.dma_start(out[n * P : (n + 1) * P, b * P : (b + 1) * P], elu[:])

@@ -112,9 +112,7 @@ def tile_graphattentionneighbournetwork_kernel(tc, h, a_src, a_dst, offs, out):
                 for d in range(DEG):
                     nc.tensor.transpose(spread_ps[:, d, :], p[:, n, d : d + 1].to_broadcast([P, P]), ident[:])
                 p_rows[b, n] = work.tile([P, P, DEG], F32, name="p_rows")
-                for k in range(BLOCK_PIECES):
-                    nodes = slice(k * PIECE_NODES, (k + 1) * PIECE_NODES)
-                    nc.scalar.copy(p_rows[b, n][:, nodes, :], spread_ps[:, :, nodes].rearrange("c d i -> c i d"))
+                nc.scalar.copy(p_rows[b, n][:], spread_ps[:].rearrange("c d i -> c i d"))
 
         for b in range(BLOCKS):
             for n in range(HEADS):

@@ -112,7 +112,9 @@ def tile_graphattentionneighbournetwork_kernel(tc, h, a_src, a_dst, offs, out):
                 for d in range(DEG):
                     nc.tensor.transpose(spread_ps[:, d, :], p[:, n, d : d + 1].to_broadcast([P, P]), ident[:])
                 p_rows[b, n] = work.tile([P, P, DEG], F32, name="p_rows")
-                nc.scalar.copy(p_rows[b, n][:], spread_ps[:].rearrange("c d i -> c i d"))
+                for k in range(BLOCK_PIECES):
+                    nodes = slice(k * PIECE_NODES, (k + 1) * PIECE_NODES)
+                    nc.scalar.copy(p_rows[b, n][:, nodes, :], spread_ps[:, :, nodes].rearrange("c d i -> c i d"))
 
         for b in range(BLOCKS):
             for n in range(HEADS):
@@ -131,12 +133,12 @@ def tile_graphattentionneighbournetwork_kernel(tc, h, a_src, a_dst, offs, out):
                         num_t[:], prod[:, :, d], ident[:], start=(d == 0), stop=(d == DEG - 1), is_transpose=True
                     )
 
-                relu_pos = work.tile([P, P], F32, name="relu_pos")
-                nc.scalar.activation(relu_pos[:], num_t[:], ACT.Relu, scale=inv_den[b][:, n : n + 1])
                 relu_neg = work.tile([P, P], F32, name="relu_neg")
                 nc.scalar.activation(relu_neg[:], num_t[:], ACT.Relu, scale=neg_inv_den[b][:, n : n + 1])
                 exp_neg = work.tile([P, P], F32, name="exp_neg")
                 nc.scalar.activation(exp_neg[:], relu_neg[:], ACT.Exp, scale=-1.0)
+                relu_pos = work.tile([P, P], F32, name="relu_pos")
+                nc.scalar.activation(relu_pos[:], num_t[:], ACT.Relu, scale=inv_den[b][:, n : n + 1])
 
                 elu_ps = psum.tile([P, P], F32, name="elu_ps", bufs=1)
                 nc.tensor.matmul(elu_ps[:], relu_pos[:], ident[:], start=True, stop=False, is_transpose=True)

@@ -36,13 +36,13 @@ def tile_graphattentionneighbournetwork_kernel(tc, h, a_src, a_dst, offs, out):
         h_sb = [held.tile([P, NODES], F32, name=f"h{n}") for n in range(HEADS)]
         nc.sync.dma_start(h_sb[0][:], h[0:P, :])
         nc.scalar.dma_start(h_sb[1][:], h[P : 2 * P, :])
-        offsets = held.tile([P, N // 16], U16, name="offsets")
-        nc.sync.dma_start(offsets[:], offs)
         src_cols = held.tile([P, HEADS], F32, name="src_cols")
         dst_cols = held.tile([P, HEADS], F32, name="dst_cols")
         with nc.allow_non_contiguous_dma(reason="256 floats, one to a partition and head"):
             nc.sync.dma_start(src_cols[:], a_src.rearrange("(n c) o -> c (n o)", n=HEADS))
             nc.scalar.dma_start(dst_cols[:], a_dst.rearrange("(n c) o -> c (n o)", n=HEADS))
+        offsets = held.tile([P, N // 16], U16, name="offsets")
+        nc.sync.dma_start(offsets[:], offs)
 
         def piece(q):
             return offsets[:, q * PIECE_COLS : (q + 1) * PIECE_COLS]

@@ -21,6 +21,7 @@ PIECE_NODES = PIECE // DEG
 PIECE_COLS = PIECE // 16
 BLOCK_PIECES = PIECES // BLOCKS
 SLOPE = 0.2
+LAST_GROUP = (BLOCKS - 1, HEADS - 1)
 
 FLOPS = 2 * 2 * HEADS * P * NODES + 2 * HEADS * P * N
 
@@ -50,24 +51,28 @@ def tile_graphattentionneighbournetwork_kernel(tc, h, a_src, a_dst, offs, out):
         ident = held.tile([P, P], F32, name="ident")
         make_identity(nc, ident[:])
 
-        src_w = held.tile([P, HEADS, HALF], BF16, name="src_w")
-        nc.vector.tensor_copy(src_w[:], src_cols[:].unsqueeze(2).to_broadcast([P, HEADS, HALF]))
-        dst_w = held.tile([P, HEADS, HALF], BF16, name="dst_w")
-        nc.vector.tensor_copy(dst_w[:], dst_cols[:].unsqueeze(2).to_broadcast([P, HEADS, HALF]))
+        src_bf = held.tile([P, HEADS], BF16, name="src_bf")
+        nc.vector.tensor_copy(src_bf[:], src_cols[:])
+        dst_bf = held.tile([P, HEADS], BF16, name="dst_bf")
+        nc.vector.tensor_copy(dst_bf[:], dst_cols[:])
         h_bf = [held.tile([P, NODES], BF16, name=f"h_bf{n}") for n in range(HEADS)]
         nc.vector.tensor_copy(h_bf[0][:], h_sb[0][:])
         nc.scalar.copy(h_bf[1][:], h_sb[1][:])
 
-        sums_ps = psum.tile([P, 2, NODES], F32, name="sums_ps", bufs=1)
-        ss_ps, sdn_ps = sums_ps[:, 0, :], sums_ps[:, 1, :]
+        ss_ps = psum.tile([P, NODES], F32, name="ss_ps", tag="early_late", bufs=1)
+        sdn_ps = psum.tile([P, NODES], F32, name="sdn_ps", bufs=1)
         for n in range(HEADS):
             half = slice(n * HALF, (n + 1) * HALF)
-            nc.tensor.matmul(ss_ps[half, :], src_w[:, n, :], h_bf[n][:], start=True, stop=True)
+            nc.tensor.matmul(
+                ss_ps[half, :], src_bf[:, n : n + 1].to_broadcast([P, HALF]), h_bf[n][:], start=True, stop=True
+            )
         for n in range(HEADS):
             half = slice(n * HALF, (n + 1) * HALF)
-            nc.tensor.matmul(sdn_ps[half, :], dst_w[:, n, :], h_bf[n][:], start=True, stop=True)
+            nc.tensor.matmul(
+                sdn_ps[half, :], dst_bf[:, n : n + 1].to_broadcast([P, HALF]), h_bf[n][:], start=True, stop=True
+            )
         sdn = held.tile([P, NODES], F32, name="sdn")
-        nc.vector.tensor_copy(sdn[:], sdn_ps)
+        nc.vector.tensor_copy(sdn[:], sdn_ps[:])
 
         z = [held.tile([P, P, DEG], F32, name=f"z{b}") for b in range(BLOCKS)]
         for q in range(PIECES):
@@ -108,9 +113,14 @@ def tile_graphattentionneighbournetwork_kernel(tc, h, a_src, a_dst, offs, out):
             nc.vector.tensor_scalar_mul(neg_inv_den[b][:], inv_den[b][:], -1.0)
 
             for n in range(HEADS):
+                weights = p[:, n, :]
+                if (b, n) == LAST_GROUP:
+                    p_over_den = small.tile([P, DEG], F32, name="p_over_den")
+                    nc.vector.tensor_scalar_mul(p_over_den[:], p[:, n, :], inv_den[b][:, n : n + 1])
+                    weights = p_over_den[:]
                 spread_ps = psum.tile([P, DEG, P], F32, name="spread_ps")
                 for d in range(DEG):
-                    nc.tensor.transpose(spread_ps[:, d, :], p[:, n, d : d + 1].to_broadcast([P, P]), ident[:])
+                    nc.tensor.transpose(spread_ps[:, d, :], weights[:, d : d + 1].to_broadcast([P, P]), ident[:])
                 p_rows[b, n] = work.tile([P, P, DEG], F32, name="p_rows")
                 for k in range(BLOCK_PIECES):
                     nodes = slice(k * PIECE_NODES, (k + 1) * PIECE_NODES)
@@ -127,6 +137,18 @@ def tile_graphattentionneighbournetwork_kernel(tc, h, a_src, a_dst, offs, out):
                         p_rows[b, n][:, nodes, :],
                         ALU.mult,
                     )
+                if (b, n) == LAST_GROUP:
+                    v = work.tile([P, P], F32, name="v")
+                    nc.vector.tensor_reduce(v[:], prod[:], axis=AXIS.X, op=ALU.add)
+                    relu_neg = work.tile([P, P], F32, name="relu_neg")
+                    nc.scalar.activation(relu_neg[:], v[:], ACT.Relu, scale=-1.0)
+                    exp_neg = work.tile([P, P], F32, name="exp_neg")
+                    nc.scalar.activation(exp_neg[:], relu_neg[:], ACT.Exp, scale=-1.0)
+                    elu = work.tile([P, P], F32, name="elu")
+                    nc.vector.scalar_tensor_tensor(elu[:], exp_neg[:], -1.0, v[:], op0=ALU.add, op1=ALU.max)
+                    nc.sync.dma_start(out[n * P : (n + 1) * P, b * P : (b + 1) * P], elu[:])
+                    continue
+
                 num_t = psum.tile([P, P], F32, name="num_t")
                 for d in range(DEG):
                     nc.tensor.matmul(
@@ -140,7 +162,7 @@ def tile_graphattentionneighbournetwork_kernel(tc, h, a_src, a_dst, offs, out):
                 relu_pos = work.tile([P, P], F32, name="relu_pos")
                 nc.scalar.activation(relu_pos[:], num_t[:], ACT.Relu, scale=inv_den[b][:, n : n + 1])
 
-                elu_ps = psum.tile([P, P], F32, name="elu_ps", bufs=1)
+                elu_ps = psum.tile([P, P], F32, name="elu_ps", tag="early_late", bufs=1)
                 nc.tensor.matmul(elu_ps[:], relu_pos[:], ident[:], start=True, stop=False, is_transpose=True)
                 nc.tensor.matmul(elu_ps[:], exp_neg[:], ident[:], start=False, stop=True, is_transpose=True)
                 elu = work.tile([P, P], F32, name="elu")

@@ -59,8 +59,8 @@ def tile_graphattentionneighbournetwork_kernel(tc, h, a_src, a_dst, offs, out):
         nc.vector.tensor_copy(h_bf[0][:], h_sb[0][:])
         nc.scalar.copy(h_bf[1][:], h_sb[1][:])
 
-        ss_ps = psum.tile([P, NODES], F32, name="ss_ps", tag="early_late", bufs=1)
-        sdn_ps = psum.tile([P, NODES], F32, name="sdn_ps", bufs=1)
+        ss_ps = psum.tile([P, NODES], F32, name="ss_ps", tag="early_late")
+        sdn_ps = psum.tile([P, NODES], F32, name="sdn_ps", tag="early_late")
         for n in range(HEADS):
             half = slice(n * HALF, (n + 1) * HALF)
             nc.tensor.matmul(
@@ -140,12 +140,12 @@ def tile_graphattentionneighbournetwork_kernel(tc, h, a_src, a_dst, offs, out):
                 if (b, n) == LAST_GROUP:
                     v = work.tile([P, P], F32, name="v")
                     nc.vector.tensor_reduce(v[:], prod[:], axis=AXIS.X, op=ALU.add)
-                    relu_neg = work.tile([P, P], F32, name="relu_neg")
-                    nc.scalar.activation(relu_neg[:], v[:], ACT.Relu, scale=-1.0)
-                    exp_neg = work.tile([P, P], F32, name="exp_neg")
-                    nc.scalar.activation(exp_neg[:], relu_neg[:], ACT.Exp, scale=-1.0)
+                    exp_v = work.tile([P, P], F32, name="exp_v", tag="relu_neg", bufs=1)
+                    nc.scalar.activation(exp_v[:], v[:], ACT.Exp)
+                    relu_less_1 = work.tile([P, P], F32, name="relu_less_1")
+                    nc.vector.tensor_scalar(relu_less_1[:], v[:], 0.0, -1.0, op0=ALU.max, op1=ALU.add)
                     elu = work.tile([P, P], F32, name="elu")
-                    nc.vector.scalar_tensor_tensor(elu[:], exp_neg[:], -1.0, v[:], op0=ALU.add, op1=ALU.max)
+                    nc.vector.scalar_tensor_tensor(elu[:], exp_v[:], 1.0, relu_less_1[:], op0=ALU.min, op1=ALU.add)
                     nc.sync.dma_start(out[n * P : (n + 1) * P, b * P : (b + 1) * P], elu[:])
                     continue
 
@@ -155,14 +155,14 @@ def tile_graphattentionneighbournetwork_kernel(tc, h, a_src, a_dst, offs, out):
                         num_t[:], prod[:, :, d], ident[:], start=(d == 0), stop=(d == DEG - 1), is_transpose=True
                     )
 
-                relu_neg = work.tile([P, P], F32, name="relu_neg")
+                relu_neg = work.tile([P, P], F32, name="relu_neg", bufs=1)
                 nc.scalar.activation(relu_neg[:], num_t[:], ACT.Relu, scale=neg_inv_den[b][:, n : n + 1])
                 exp_neg = work.tile([P, P], F32, name="exp_neg")
                 nc.scalar.activation(exp_neg[:], relu_neg[:], ACT.Exp, scale=-1.0)
                 relu_pos = work.tile([P, P], F32, name="relu_pos")
                 nc.scalar.activation(relu_pos[:], num_t[:], ACT.Relu, scale=inv_den[b][:, n : n + 1])
 
-                elu_ps = psum.tile([P, P], F32, name="elu_ps", tag="early_late", bufs=1)
+                elu_ps = psum.tile([P, P], F32, name="elu_ps", tag="early_late")
                 nc.tensor.matmul(elu_ps[:], relu_pos[:], ident[:], start=True, stop=False, is_transpose=True)
                 nc.tensor.matmul(elu_ps[:], exp_neg[:], ident[:], start=False, stop=True, is_transpose=True)
                 elu = work.tile([P, P], F32, name="elu")

@@ -34,14 +34,16 @@ def tile_graphattentionneighbournetwork_kernel(tc, h, a_src, a_dst, offs, out):
         tc.tile_pool(name="work", bufs=BLOCKS * HEADS) as work,
         tc.psum_pool(name="psum", bufs=2) as psum,
     ):
-        h_sb = [held.tile([P, NODES], F32, name=f"h{n}") for n in range(HEADS)]
-        nc.sync.dma_start(h_sb[0][:], h[0:P, :])
-        nc.scalar.dma_start(h_sb[1][:], h[P : 2 * P, :])
         src_cols = held.tile([P, HEADS], F32, name="src_cols")
         dst_cols = held.tile([P, HEADS], F32, name="dst_cols")
         with nc.allow_non_contiguous_dma(reason="256 floats, one to a partition and head"):
             nc.sync.dma_start(src_cols[:], a_src.rearrange("(n c) o -> c (n o)", n=HEADS))
             nc.scalar.dma_start(dst_cols[:], a_dst.rearrange("(n c) o -> c (n o)", n=HEADS))
+        h_sb = [held.tile([P, NODES], F32, name=f"h{n}") for n in range(HEADS)]
+        for b in range(BLOCKS):
+            cols = slice(b * P, (b + 1) * P)
+            nc.sync.dma_start(h_sb[0][:, cols], h[0:P, cols])
+            nc.scalar.dma_start(h_sb[1][:, cols], h[P : 2 * P, cols])
         offsets = held.tile([P, N // 16], U16, name="offsets")
         nc.sync.dma_start(offsets[:], offs)
 
@@ -56,23 +58,26 @@ def tile_graphattentionneighbournetwork_kernel(tc, h, a_src, a_dst, offs, out):
         dst_bf = held.tile([P, HEADS], BF16, name="dst_bf")
         nc.vector.tensor_copy(dst_bf[:], dst_cols[:])
         h_bf = [held.tile([P, NODES], BF16, name=f"h_bf{n}") for n in range(HEADS)]
-        nc.vector.tensor_copy(h_bf[0][:], h_sb[0][:])
-        nc.scalar.copy(h_bf[1][:], h_sb[1][:])
+        for b in range(BLOCKS):
+            cols = slice(b * P, (b + 1) * P)
+            nc.vector.tensor_copy(h_bf[0][:, cols], h_sb[0][:, cols])
+            nc.scalar.copy(h_bf[1][:, cols], h_sb[1][:, cols])
 
-        ss_ps = psum.tile([P, NODES], F32, name="ss_ps", tag="early_late")
-        sdn_ps = psum.tile([P, NODES], F32, name="sdn_ps", tag="early_late")
-        for n in range(HEADS):
-            half = slice(n * HALF, (n + 1) * HALF)
-            nc.tensor.matmul(
-                ss_ps[half, :], src_bf[:, n : n + 1].to_broadcast([P, HALF]), h_bf[n][:], start=True, stop=True
-            )
-        for n in range(HEADS):
-            half = slice(n * HALF, (n + 1) * HALF)
-            nc.tensor.matmul(
-                sdn_ps[half, :], dst_bf[:, n : n + 1].to_broadcast([P, HALF]), h_bf[n][:], start=True, stop=True
-            )
+        ss_ps = [psum.tile([P, P], F32, name=f"ss_ps{b}", tag="early_late") for b in range(BLOCKS)]
+        sdn_ps = [psum.tile([P, P], F32, name=f"sdn_ps{b}", tag="num_t") for b in range(BLOCKS)]
         sdn = held.tile([P, NODES], F32, name="sdn")
-        nc.vector.tensor_copy(sdn[:], sdn_ps[:])
+        for b in range(BLOCKS):
+            cols = slice(b * P, (b + 1) * P)
+            for sums_ps, vector_bf in ((sdn_ps[b], dst_bf), (ss_ps[b], src_bf)):
+                for n in range(HEADS):
+                    nc.tensor.matmul(
+                        sums_ps[n * HALF : (n + 1) * HALF, :],
+                        vector_bf[:, n : n + 1].to_broadcast([P, HALF]),
+                        h_bf[n][:, cols],
+                        start=True,
+                        stop=True,
+                    )
+            nc.vector.tensor_copy(sdn[:, cols], sdn_ps[b][:])
 
         z = [held.tile([P, P, DEG], F32, name=f"z{b}") for b in range(BLOCKS)]
         for q in range(PIECES):
@@ -80,7 +85,7 @@ def tile_graphattentionneighbournetwork_kernel(tc, h, a_src, a_dst, offs, out):
             ss_rep = work.tile([P, PIECE_NODES, DEG], F32, name="ss_rep")
             nc.scalar.copy(
                 ss_rep[:],
-                ss_ps[:, q * PIECE_NODES : (q + 1) * PIECE_NODES].unsqueeze(2).to_broadcast([P, PIECE_NODES, DEG]),
+                ss_ps[b][:, k * PIECE_NODES : (k + 1) * PIECE_NODES].unsqueeze(2).to_broadcast([P, PIECE_NODES, DEG]),
             )
             nc.vector.tensor_tensor(
                 z[b][:, k * PIECE_NODES : (k + 1) * PIECE_NODES, :], sdn[:].indirect(piece(q)), ss_rep[:], ALU.add
@@ -146,7 +151,7 @@ def tile_graphattentionneighbournetwork_kernel(tc, h, a_src, a_dst, offs, out):
                     nc.vector.tensor_scalar(relu_less_1[:], v[:], 0.0, -1.0, op0=ALU.max, op1=ALU.add)
                     elu = work.tile([P, P], F32, name="elu")
                     nc.vector.scalar_tensor_tensor(elu[:], exp_v[:], 1.0, relu_less_1[:], op0=ALU.min, op1=ALU.add)
-                    nc.sync.dma_start(out[n * P : (n + 1) * P, b * P : (b + 1) * P], elu[:])
+                    nc.scalar.dma_start(out[n * P : (n + 1) * P, b * P : (b + 1) * P], elu[:])
                     continue
 
                 num_t = psum.tile([P, P], F32, name="num_t")

@@ -123,7 +123,7 @@ def tile_graphattentionneighbournetwork_kernel(tc, h, a_src, a_dst, offs, out):
                     p_over_den = small.tile([P, DEG], F32, name="p_over_den")
                     nc.vector.tensor_scalar_mul(p_over_den[:], p[:, n, :], inv_den[b][:, n : n + 1])
                     weights = p_over_den[:]
-                spread_ps = psum.tile([P, DEG, P], F32, name="spread_ps")
+                spread_ps = psum.tile([P, DEG, P], F32, name="spread_ps", tag=("num_t" if b == 0 else "spread_ps"))
                 for d in range(DEG):
                     nc.tensor.transpose(spread_ps[:, d, :], weights[:, d : d + 1].to_broadcast([P, P]), ident[:])
                 p_rows[b, n] = work.tile([P, P, DEG], F32, name="p_rows")

@@ -131,45 +131,58 @@ def tile_graphattentionneighbournetwork_kernel(tc, h, a_src, a_dst, offs, out):
                     nodes = slice(k * PIECE_NODES, (k + 1) * PIECE_NODES)
                     nc.scalar.copy(p_rows[b, n][:, nodes, :], spread_ps[:, :, nodes].rearrange("c d i -> c i d"))
 
-        for b in range(BLOCKS):
-            for n in range(HEADS):
-                prod = work.tile([P, P, DEG], F32, name="prod")
-                for k in range(BLOCK_PIECES):
-                    nodes = slice(k * PIECE_NODES, (k + 1) * PIECE_NODES)
-                    nc.vector.tensor_tensor(
-                        prod[:, nodes, :],
-                        h_sb[n][:].indirect(piece(b * BLOCK_PIECES + k)),
-                        p_rows[b, n][:, nodes, :],
-                        ALU.mult,
-                    )
-                if (b, n) == LAST_GROUP:
-                    v = work.tile([P, P], F32, name="v")
-                    nc.vector.tensor_reduce(v[:], prod[:], axis=AXIS.X, op=ALU.add)
-                    exp_v = work.tile([P, P], F32, name="exp_v", tag="relu_neg", bufs=1)
-                    nc.scalar.activation(exp_v[:], v[:], ACT.Exp)
-                    relu_less_1 = work.tile([P, P], F32, name="relu_less_1")
-                    nc.vector.tensor_scalar(relu_less_1[:], v[:], 0.0, -1.0, op0=ALU.max, op1=ALU.add)
-                    elu = work.tile([P, P], F32, name="elu")
-                    nc.vector.scalar_tensor_tensor(elu[:], exp_v[:], 1.0, relu_less_1[:], op0=ALU.min, op1=ALU.add)
-                    nc.scalar.dma_start(out[n * P : (n + 1) * P, b * P : (b + 1) * P], elu[:])
-                    continue
+        def multiply(b, n):
+            prod = work.tile([P, P, DEG], F32, name="prod")
+            for k in range(BLOCK_PIECES):
+                nodes = slice(k * PIECE_NODES, (k + 1) * PIECE_NODES)
+                nc.vector.tensor_tensor(
+                    prod[:, nodes, :],
+                    h_sb[n][:].indirect(piece(b * BLOCK_PIECES + k)),
+                    p_rows[b, n][:, nodes, :],
+                    ALU.mult,
+                )
+            return prod
 
-                num_t = psum.tile([P, P], F32, name="num_t")
-                for d in range(DEG):
-                    nc.tensor.matmul(
-                        num_t[:], prod[:, :, d], ident[:], start=(d == 0), stop=(d == DEG - 1), is_transpose=True
-                    )
+        def finish_through_tensor(b, n, prod, last_copy_on_vector):
+            num_t = psum.tile([P, P], F32, name="num_t")
+            for d in range(DEG):
+                nc.tensor.matmul(
+                    num_t[:], prod[:, :, d], ident[:], start=(d == 0), stop=(d == DEG - 1), is_transpose=True
+                )
 
-                relu_neg = work.tile([P, P], F32, name="relu_neg", bufs=1)
-                nc.scalar.activation(relu_neg[:], num_t[:], ACT.Relu, scale=neg_inv_den[b][:, n : n + 1])
-                exp_neg = work.tile([P, P], F32, name="exp_neg")
-                nc.scalar.activation(exp_neg[:], relu_neg[:], ACT.Exp, scale=-1.0)
-                relu_pos = work.tile([P, P], F32, name="relu_pos")
-                nc.scalar.activation(relu_pos[:], num_t[:], ACT.Relu, scale=inv_den[b][:, n : n + 1])
+            relu_neg = work.tile([P, P], F32, name="relu_neg", bufs=1)
+            nc.scalar.activation(relu_neg[:], num_t[:], ACT.Relu, scale=neg_inv_den[b][:, n : n + 1])
+            exp_neg = work.tile([P, P], F32, name="exp_neg")
+            nc.scalar.activation(exp_neg[:], relu_neg[:], ACT.Exp, scale=-1.0)
+            relu_pos = work.tile([P, P], F32, name="relu_pos")
+            nc.scalar.activation(relu_pos[:], num_t[:], ACT.Relu, scale=inv_den[b][:, n : n + 1])
 
-                elu_ps = psum.tile([P, P], F32, name="elu_ps", tag="early_late")
-                nc.tensor.matmul(elu_ps[:], relu_pos[:], ident[:], start=True, stop=False, is_transpose=True)
-                nc.tensor.matmul(elu_ps[:], exp_neg[:], ident[:], start=False, stop=True, is_transpose=True)
-                elu = work.tile([P, P], F32, name="elu")
+            elu_ps = psum.tile([P, P], F32, name="elu_ps", tag="early_late")
+            nc.tensor.matmul(elu_ps[:], relu_pos[:], ident[:], start=True, stop=False, is_transpose=True)
+            nc.tensor.matmul(elu_ps[:], exp_neg[:], ident[:], start=False, stop=True, is_transpose=True)
+            elu = work.tile([P, P], F32, name="elu")
+            if last_copy_on_vector:
+                nc.vector.tensor_scalar_add(elu[:], elu_ps[:], -1.0)
+            else:
                 nc.scalar.add(elu[:], elu_ps[:], -1.0)
-                nc.sync.dma_start(out[n * P : (n + 1) * P, b * P : (b + 1) * P], elu[:])
+            nc.sync.dma_start(out[n * P : (n + 1) * P, b * P : (b + 1) * P], elu[:])
+
+        groups = [(b, n) for b in range(BLOCKS) for n in range(HEADS)]
+        prods = {}
+        for group in groups:
+            prods[group] = multiply(*group)
+
+        v = work.tile([P, P], F32, name="v")
+        nc.vector.tensor_reduce(v[:], prods[LAST_GROUP][:], axis=AXIS.X, op=ALU.add)
+
+        for g, group in enumerate(groups[:-1]):
+            finish_through_tensor(*group, prods[group], g == 1)
+
+        b, n = LAST_GROUP
+        exp_v = work.tile([P, P], F32, name="exp_v", tag="relu_neg", bufs=1)
+        nc.scalar.activation(exp_v[:], v[:], ACT.Exp)
+        relu_less_1 = work.tile([P, P], F32, name="relu_less_1")
+        nc.vector.tensor_scalar(relu_less_1[:], v[:], 0.0, -1.0, op0=ALU.max, op1=ALU.add)
+        elu = work.tile([P, P], F32, name="elu")
+        nc.vector.scalar_tensor_tensor(elu[:], exp_v[:], 1.0, relu_less_1[:], op0=ALU.min, op1=ALU.add)
+        nc.scalar.dma_start(out[n * P : (n + 1) * P, b * P : (b + 1) * P], elu[:])

import concourse.mybir as mybir
from concourse.masks import make_identity

F32 = mybir.dt.float32
BF16 = mybir.dt.bfloat16
U16 = mybir.dt.uint16
ALU = mybir.AluOpType
ACT = mybir.ActivationFunctionType
AXIS = mybir.AxisListType

P = 128
HEADS = 2
HALF = P // HEADS
NODES = 256
BLOCKS = NODES // P
DEG = 4
N = NODES * DEG
PIECE = 256
PIECES = N // PIECE
PIECE_NODES = PIECE // DEG
PIECE_COLS = PIECE // 16
BLOCK_PIECES = PIECES // BLOCKS
SLOPE = 0.2
LAST_GROUP = (BLOCKS - 1, HEADS - 1)

FLOPS = 2 * 2 * HEADS * P * NODES + 2 * HEADS * P * N


def tile_graphattentionneighbournetwork_kernel(tc, h, a_src, a_dst, offs, out):
    nc = tc.nc
    with (
        tc.tile_pool(name="held", bufs=1) as held,
        tc.tile_pool(name="small", bufs=BLOCKS) as small,
        tc.tile_pool(name="work", bufs=BLOCKS * HEADS) as work,
        tc.psum_pool(name="psum", bufs=2) as psum,
    ):
        src_cols = held.tile([P, HEADS], F32, name="src_cols")
        dst_cols = held.tile([P, HEADS], F32, name="dst_cols")
        with nc.allow_non_contiguous_dma(reason="256 floats, one to a partition and head"):
            nc.sync.dma_start(src_cols[:], a_src.rearrange("(n c) o -> c (n o)", n=HEADS))
            nc.scalar.dma_start(dst_cols[:], a_dst.rearrange("(n c) o -> c (n o)", n=HEADS))
        h_sb = [held.tile([P, NODES], F32, name=f"h{n}") for n in range(HEADS)]
        for b in range(BLOCKS):
            cols = slice(b * P, (b + 1) * P)
            nc.sync.dma_start(h_sb[0][:, cols], h[0:P, cols])
            nc.scalar.dma_start(h_sb[1][:, cols], h[P : 2 * P, cols])
        offsets = held.tile([P, N // 16], U16, name="offsets")
        nc.sync.dma_start(offsets[:], offs)

        def piece(q):
            return offsets[:, q * PIECE_COLS : (q + 1) * PIECE_COLS]

        ident = held.tile([P, P], F32, name="ident")
        make_identity(nc, ident[:])

        src_bf = held.tile([P, HEADS], BF16, name="src_bf")
        nc.vector.tensor_copy(src_bf[:], src_cols[:])
        dst_bf = held.tile([P, HEADS], BF16, name="dst_bf")
        nc.vector.tensor_copy(dst_bf[:], dst_cols[:])
        h_bf = [held.tile([P, NODES], BF16, name=f"h_bf{n}") for n in range(HEADS)]
        for b in range(BLOCKS):
            cols = slice(b * P, (b + 1) * P)
            nc.vector.tensor_copy(h_bf[0][:, cols], h_sb[0][:, cols])
            nc.scalar.copy(h_bf[1][:, cols], h_sb[1][:, cols])

        ss_ps = [psum.tile([P, P], F32, name=f"ss_ps{b}", tag="early_late") for b in range(BLOCKS)]
        sdn_ps = [psum.tile([P, P], F32, name=f"sdn_ps{b}", tag="num_t") for b in range(BLOCKS)]
        sdn = held.tile([P, NODES], F32, name="sdn")
        for b in range(BLOCKS):
            cols = slice(b * P, (b + 1) * P)
            for sums_ps, vector_bf in ((sdn_ps[b], dst_bf), (ss_ps[b], src_bf)):
                for n in range(HEADS):
                    nc.tensor.matmul(
                        sums_ps[n * HALF : (n + 1) * HALF, :],
                        vector_bf[:, n : n + 1].to_broadcast([P, HALF]),
                        h_bf[n][:, cols],
                        start=True,
                        stop=True,
                    )
            nc.vector.tensor_copy(sdn[:, cols], sdn_ps[b][:])

        z = [held.tile([P, P, DEG], F32, name=f"z{b}") for b in range(BLOCKS)]
        for q in range(PIECES):
            b, k = divmod(q, BLOCK_PIECES)
            ss_rep = work.tile([P, PIECE_NODES, DEG], F32, name="ss_rep")
            nc.scalar.copy(
                ss_rep[:],
                ss_ps[b][:, k * PIECE_NODES : (k + 1) * PIECE_NODES].unsqueeze(2).to_broadcast([P, PIECE_NODES, DEG]),
            )
            nc.vector.tensor_tensor(
                z[b][:, k * PIECE_NODES : (k + 1) * PIECE_NODES, :], sdn[:].indirect(piece(q)), ss_rep[:], ALU.add
            )

        p_rows, inv_den, neg_inv_den = {}, [], []
        for b in range(BLOCKS):
            z_t = psum.tile([P, DEG, HEADS, HALF], F32, name="z_t")
            for d in range(DEG):
                nc.tensor.transpose(z_t[:, d, :, :].rearrange("i n k -> i (n k)"), z[b][:, :, d], ident[:])
            scores = z_t[:, :, :, 0].rearrange("i d n -> i n d")

            scaled = small.tile([P, HEADS, DEG], F32, name="scaled")
            nc.vector.tensor_scalar_mul(scaled[:], scores, SLOPE)
            neg_max = small.tile([P, HEADS], F32, name="neg_max")
            nc.vector.tensor_reduce(neg_max[:], scores, axis=AXIS.X, op=ALU.max, negate=True)
            lrelu = small.tile([P, HEADS, DEG], F32, name="lrelu")
            nc.vector.tensor_tensor(lrelu[:], scaled[:], scores, ALU.max)
            neg_top = small.tile([P, HEADS], F32, name="neg_top")
            nc.vector.scalar_tensor_tensor(neg_top[:], neg_max[:], SLOPE, neg_max[:], op0=ALU.mult, op1=ALU.min)
            p = small.tile([P, HEADS, DEG], F32, name="p")
            den = small.tile([P, HEADS], F32, name="den")
            for n in range(HEADS):
                nc.scalar.activation(
                    p[:, n, :], lrelu[:, n, :], ACT.Exp, bias=neg_top[:, n : n + 1], accum_out=den[:, n : n + 1]
                )
            inv_den.append(small.tile([P, HEADS], F32, name="inv_den"))
            nc.vector.reciprocal(inv_den[b][:], den[:])
            neg_inv_den.append(small.tile([P, HEADS], F32, name="neg_inv_den"))
            nc.vector.tensor_scalar_mul(neg_inv_den[b][:], inv_den[b][:], -1.0)

            for n in range(HEADS):
                weights = p[:, n, :]
                if (b, n) == LAST_GROUP:
                    p_over_den = small.tile([P, DEG], F32, name="p_over_den")
                    nc.vector.tensor_scalar_mul(p_over_den[:], p[:, n, :], inv_den[b][:, n : n + 1])
                    weights = p_over_den[:]
                spread_ps = psum.tile([P, DEG, P], F32, name="spread_ps", tag=("num_t" if b == 0 else "spread_ps"))
                for d in range(DEG):
                    nc.tensor.transpose(spread_ps[:, d, :], weights[:, d : d + 1].to_broadcast([P, P]), ident[:])
                p_rows[b, n] = work.tile([P, P, DEG], F32, name="p_rows")
                for k in range(BLOCK_PIECES):
                    nodes = slice(k * PIECE_NODES, (k + 1) * PIECE_NODES)
                    nc.scalar.copy(p_rows[b, n][:, nodes, :], spread_ps[:, :, nodes].rearrange("c d i -> c i d"))

        def multiply(b, n):
            prod = work.tile([P, P, DEG], F32, name="prod")
            for k in range(BLOCK_PIECES):
                nodes = slice(k * PIECE_NODES, (k + 1) * PIECE_NODES)
                nc.vector.tensor_tensor(
                    prod[:, nodes, :],
                    h_sb[n][:].indirect(piece(b * BLOCK_PIECES + k)),
                    p_rows[b, n][:, nodes, :],
                    ALU.mult,
                )
            return prod

        def finish_through_tensor(b, n, prod, last_copy_on_vector):
            num_t = psum.tile([P, P], F32, name="num_t")
            for d in range(DEG):
                nc.tensor.matmul(
                    num_t[:], prod[:, :, d], ident[:], start=(d == 0), stop=(d == DEG - 1), is_transpose=True
                )

            relu_neg = work.tile([P, P], F32, name="relu_neg", bufs=1)
            nc.scalar.activation(relu_neg[:], num_t[:], ACT.Relu, scale=neg_inv_den[b][:, n : n + 1])
            exp_neg = work.tile([P, P], F32, name="exp_neg")
            nc.scalar.activation(exp_neg[:], relu_neg[:], ACT.Exp, scale=-1.0)
            relu_pos = work.tile([P, P], F32, name="relu_pos")
            nc.scalar.activation(relu_pos[:], num_t[:], ACT.Relu, scale=inv_den[b][:, n : n + 1])

            elu_ps = psum.tile([P, P], F32, name="elu_ps", tag="early_late")
            nc.tensor.matmul(elu_ps[:], relu_pos[:], ident[:], start=True, stop=False, is_transpose=True)
            nc.tensor.matmul(elu_ps[:], exp_neg[:], ident[:], start=False, stop=True, is_transpose=True)
            elu = work.tile([P, P], F32, name="elu")
            if last_copy_on_vector:
                nc.vector.tensor_scalar_add(elu[:], elu_ps[:], -1.0)
            else:
                nc.scalar.add(elu[:], elu_ps[:], -1.0)
            nc.sync.dma_start(out[n * P : (n + 1) * P, b * P : (b + 1) * P], elu[:])

        groups = [(b, n) for b in range(BLOCKS) for n in range(HEADS)]
        prods = {}
        for group in groups:
            prods[group] = multiply(*group)

        v = work.tile([P, P], F32, name="v")
        nc.vector.tensor_reduce(v[:], prods[LAST_GROUP][:], axis=AXIS.X, op=ALU.add)

        for g, group in enumerate(groups[:-1]):
            finish_through_tensor(*group, prods[group], g == 1)

        b, n = LAST_GROUP
        exp_v = work.tile([P, P], F32, name="exp_v", tag="relu_neg", bufs=1)
        nc.scalar.activation(exp_v[:], v[:], ACT.Exp)
        relu_less_1 = work.tile([P, P], F32, name="relu_less_1")
        nc.vector.tensor_scalar(relu_less_1[:], v[:], 0.0, -1.0, op0=ALU.max, op1=ALU.add)
        elu = work.tile([P, P], F32, name="elu")
        nc.vector.scalar_tensor_tensor(elu[:], exp_v[:], 1.0, relu_less_1[:], op0=ALU.min, op1=ALU.add)
        nc.scalar.dma_start(out[n * P : (n + 1) * P, b * P : (b + 1) * P], elu[:])
